import numpy as np
import ml_dtypes

BF16 = ml_dtypes.bfloat16


def bf(x):
    return np.asarray(x, np.float32).astype(BF16)


def f32(x):
    return np.asarray(x, np.float32)


def f64(x):
    return np.asarray(x).astype(np.float64)


def striped(idx):
    return np.tile(idx.reshape(-1, 16).T, (8, 1))


D, S, M, N = 128, 256, 256, 128


def sigmoid(v):
    return 1.0 / (1.0 + np.exp(-v))


def setup_inputs():
    return {"table": bf(0.5 * np.random.standard_normal((D, S))), "w": bf(0.16 * np.random.standard_normal((D, M))), "b": f32(0.3 * np.random.standard_normal((M, 1))), "offs": striped(np.random.permutation(np.tile(np.arange(S), 2))[:N])}


def reference(table, w, b, offs):
    idx = offs[:16].T.reshape(-1)
    z = f64(w).T @ f64(table)[:, idx] + f64(b)
    c = z[:D]
    h = sigmoid(z[D:]) * np.tanh(c)
    return np.concatenate([c, h], axis=0)

@@ -1,0 +1,44 @@
+import concourse.mybir as mybir
+
+BF16, F32, U16 = mybir.dt.bfloat16, mybir.dt.float32, mybir.dt.uint16
+SIGMOID = mybir.ActivationFunctionType.Sigmoid
+TANH = mybir.ActivationFunctionType.Tanh
+
+P = 128
+NODES = 256
+LEAVES = 128
+FLOPS = 2 * P * (2 * P) * LEAVES
+
+
+def tile_logicencoder_kernel(tc, table, w, b, offs, out):
+    nc = tc.nc
+    with (
+        tc.tile_pool(name="held", bufs=1) as held,
+        tc.psum_pool(name="psum", bufs=1) as psum,
+    ):
+        offsets = held.tile([P, LEAVES // 16], U16, name="offsets")
+        nc.sync.dma_start(offsets[:], offs)
+        nodes = held.tile([P, NODES], BF16, name="nodes")
+        nc.sync.dma_start(nodes[:], table)
+        weights = held.tile([P, 2 * P], BF16, name="weights")
+        nc.scalar.dma_start(weights[:], w)
+        bias = held.tile([P, 2], F32, name="bias")
+        with nc.allow_non_contiguous_dma(reason="256 bias values, one to a partition and column"):
+            nc.scalar.dma_start(bias[:], b.rearrange("(h m) o -> m (h o)", h=2))
+
+        cell_sum = psum.tile([P, LEAVES], F32, name="cell_sum")
+        nc.tensor.matmul(cell_sum[:], weights[:, 0:P], nodes[:].indirect(offsets[:]), start=True, stop=True)
+        gate_sum = psum.tile([P, LEAVES], F32, name="gate_sum")
+        nc.tensor.matmul(gate_sum[:], weights[:, P : 2 * P], nodes[:].indirect(offsets[:]), start=True, stop=True)
+
+        cell = held.tile([P, LEAVES], F32, name="cell")
+        nc.vector.tensor_scalar_add(cell[:], cell_sum[:], bias[:, 0:1])
+        nc.sync.dma_start(out[0:P, :], cell[:])
+
+        gate = held.tile([P, LEAVES], F32, name="gate")
+        nc.scalar.activation(gate[:], gate_sum[:], SIGMOID, bias=bias[:, 1:2])
+        squashed = held.tile([P, LEAVES], F32, name="squashed")
+        nc.scalar.activation(squashed[:], cell[:], TANH)
+        hidden = held.tile([P, LEAVES], F32, name="hidden")
+        nc.vector.tensor_mul(hidden[:], gate[:], squashed[:])
+        nc.sync.dma_start(out[P : 2 * P, :], hidden[:])

@@ -26,6 +26,10 @@ def tile_logicencoder_kernel(tc, table, w, b, offs, out):
         with nc.allow_non_contiguous_dma(reason="256 bias values, one to a partition and column"):
             nc.scalar.dma_start(bias[:], b.rearrange("(h m) o -> m (h o)", h=2))
 
+        scratch = held.tile([P, 1], F32, name="scratch")
+        nc.vector.memset(scratch[:], 0.0)
+        nc.scalar.activation(scratch[:], scratch[:], SIGMOID)
+
         cell_sum = psum.tile([P, LEAVES], F32, name="cell_sum")
         nc.tensor.matmul(cell_sum[:], weights[:, 0:P], nodes[:].indirect(offsets[:]), start=True, stop=True)
         gate_sum = psum.tile([P, LEAVES], F32, name="gate_sum")

@@ -20,15 +20,28 @@ def tile_logicencoder_kernel(tc, table, w, b, offs, out):
         nc.sync.dma_start(offsets[:], offs)
         nodes = held.tile([P, NODES], BF16, name="nodes")
         nc.sync.dma_start(nodes[:], table)
+        bias_row = held.tile([1, 2 * P], F32, name="bias_row")
+        nc.scalar.dma_start(bias_row[:], b.rearrange("m o -> o m"))
         weights = held.tile([P, 2 * P], BF16, name="weights")
         nc.scalar.dma_start(weights[:], w)
-        bias = held.tile([P, 2], F32, name="bias")
-        with nc.allow_non_contiguous_dma(reason="256 bias values, one to a partition and column"):
-            nc.scalar.dma_start(bias[:], b.rearrange("(h m) o -> m (h o)", h=2))
 
         scratch = held.tile([P, 1], F32, name="scratch")
         nc.vector.memset(scratch[:], 0.0)
         nc.scalar.activation(scratch[:], scratch[:], SIGMOID)
+
+        one = held.tile([1, 1], F32, name="one")
+        nc.vector.memset(one[:], 1.0)
+        bias_columns = psum.tile([P, 2], F32, name="bias_columns")
+        for half in range(2):
+            nc.tensor.matmul(
+                bias_columns[:, half : half + 1],
+                bias_row[:, half * P : (half + 1) * P],
+                one[:],
+                start=True,
+                stop=True,
+            )
+        bias = held.tile([P, 2], F32, name="bias")
+        nc.vector.tensor_copy(bias[:], bias_columns[:])
 
         cell_sum = psum.tile([P, LEAVES], F32, name="cell_sum")
         nc.tensor.matmul(cell_sum[:], weights[:, 0:P], nodes[:].indirect(offsets[:]), start=True, stop=True)

@@ -3,6 +3,7 @@ import concourse.mybir as mybir
 BF16, F32, U16 = mybir.dt.bfloat16, mybir.dt.float32, mybir.dt.uint16
 SIGMOID = mybir.ActivationFunctionType.Sigmoid
 TANH = mybir.ActivationFunctionType.Tanh
+IDENTITY = mybir.ActivationFunctionType.Identity
 
 P = 128
 NODES = 256
@@ -20,42 +21,29 @@ def tile_logicencoder_kernel(tc, table, w, b, offs, out):
         nc.sync.dma_start(offsets[:], offs)
         nodes = held.tile([P, NODES], BF16, name="nodes")
         nc.sync.dma_start(nodes[:], table)
-        bias_row = held.tile([1, 2 * P], F32, name="bias_row")
-        nc.scalar.dma_start(bias_row[:], b.rearrange("m o -> o m"))
         weights = held.tile([P, 2 * P], BF16, name="weights")
         nc.scalar.dma_start(weights[:], w)
+        bias = held.tile([P, 2], F32, name="bias")
+        with nc.allow_non_contiguous_dma(reason="256 bias values, one to a partition and column"):
+            nc.scalar.dma_start(bias[:], b.rearrange("(h m) o -> m (h o)", h=2))
 
         scratch = held.tile([P, 1], F32, name="scratch")
         nc.vector.memset(scratch[:], 0.0)
         nc.scalar.activation(scratch[:], scratch[:], SIGMOID)
-
-        one = held.tile([1, 1], F32, name="one")
-        nc.vector.memset(one[:], 1.0)
-        bias_columns = psum.tile([P, 2], F32, name="bias_columns")
-        for half in range(2):
-            nc.tensor.matmul(
-                bias_columns[:, half : half + 1],
-                bias_row[:, half * P : (half + 1) * P],
-                one[:],
-                start=True,
-                stop=True,
-            )
-        bias = held.tile([P, 2], F32, name="bias")
-        nc.vector.tensor_copy(bias[:], bias_columns[:])
 
         cell_sum = psum.tile([P, LEAVES], F32, name="cell_sum")
         nc.tensor.matmul(cell_sum[:], weights[:, 0:P], nodes[:].indirect(offsets[:]), start=True, stop=True)
         gate_sum = psum.tile([P, LEAVES], F32, name="gate_sum")
         nc.tensor.matmul(gate_sum[:], weights[:, P : 2 * P], nodes[:].indirect(offsets[:]), start=True, stop=True)
 
+        squashed = held.tile([P, LEAVES], F32, name="squashed")
+        nc.scalar.activation(squashed[:], cell_sum[:], TANH, bias=bias[:, 0:1])
         cell = held.tile([P, LEAVES], F32, name="cell")
-        nc.vector.tensor_scalar_add(cell[:], cell_sum[:], bias[:, 0:1])
-        nc.sync.dma_start(out[0:P, :], cell[:])
-
+        nc.scalar.activation(cell[:], cell_sum[:], IDENTITY, bias=bias[:, 0:1])
+        nc.scalar.dma_start(out[0:P, :], cell[:])
         gate = held.tile([P, LEAVES], F32, name="gate")
         nc.scalar.activation(gate[:], gate_sum[:], SIGMOID, bias=bias[:, 1:2])
-        squashed = held.tile([P, LEAVES], F32, name="squashed")
-        nc.scalar.activation(squashed[:], cell[:], TANH)
+
         hidden = held.tile([P, LEAVES], F32, name="hidden")
         nc.vector.tensor_mul(hidden[:], gate[:], squashed[:])
         nc.sync.dma_start(out[P : 2 * P, :], hidden[:])

@@ -40,7 +40,7 @@ def tile_logicencoder_kernel(tc, table, w, b, offs, out):
         nc.scalar.activation(squashed[:], cell_sum[:], TANH, bias=bias[:, 0:1])
         cell = held.tile([P, LEAVES], F32, name="cell")
         nc.scalar.activation(cell[:], cell_sum[:], IDENTITY, bias=bias[:, 0:1])
-        nc.scalar.dma_start(out[0:P, :], cell[:])
+        nc.sync.dma_start(out[0:P, :], cell[:])
         gate = held.tile([P, LEAVES], F32, name="gate")
         nc.scalar.activation(gate[:], gate_sum[:], SIGMOID, bias=bias[:, 1:2])
 

@@ -23,9 +23,10 @@ def tile_logicencoder_kernel(tc, table, w, b, offs, out):
         nc.sync.dma_start(nodes[:], table)
         weights = held.tile([P, 2 * P], BF16, name="weights")
         nc.scalar.dma_start(weights[:], w)
-        bias = held.tile([P, 2], F32, name="bias")
-        with nc.allow_non_contiguous_dma(reason="256 bias values, one to a partition and column"):
-            nc.scalar.dma_start(bias[:], b.rearrange("(h m) o -> m (h o)", h=2))
+        cell_bias = held.tile([P, 1], F32, name="cell_bias")
+        nc.scalar.dma_start(cell_bias[:], b[0:P, :])
+        gate_bias = held.tile([P, 1], F32, name="gate_bias")
+        nc.sync.dma_start(gate_bias[:], b[P : 2 * P, :])
 
         scratch = held.tile([P, 1], F32, name="scratch")
         nc.vector.memset(scratch[:], 0.0)
@@ -37,12 +38,12 @@ def tile_logicencoder_kernel(tc, table, w, b, offs, out):
         nc.tensor.matmul(gate_sum[:], weights[:, P : 2 * P], nodes[:].indirect(offsets[:]), start=True, stop=True)
 
         squashed = held.tile([P, LEAVES], F32, name="squashed")
-        nc.scalar.activation(squashed[:], cell_sum[:], TANH, bias=bias[:, 0:1])
+        nc.scalar.activation(squashed[:], cell_sum[:], TANH, bias=cell_bias[:])
         cell = held.tile([P, LEAVES], F32, name="cell")
-        nc.scalar.activation(cell[:], cell_sum[:], IDENTITY, bias=bias[:, 0:1])
+        nc.scalar.activation(cell[:], cell_sum[:], IDENTITY, bias=cell_bias[:])
         nc.sync.dma_start(out[0:P, :], cell[:])
         gate = held.tile([P, LEAVES], F32, name="gate")
-        nc.scalar.activation(gate[:], gate_sum[:], SIGMOID, bias=bias[:, 1:2])
+        nc.scalar.activation(gate[:], gate_sum[:], SIGMOID, bias=gate_bias[:])
 
         hidden = held.tile([P, LEAVES], F32, name="hidden")
         nc.vector.tensor_mul(hidden[:], gate[:], squashed[:])

@@ -21,12 +21,11 @@ def tile_logicencoder_kernel(tc, table, w, b, offs, out):
         nc.sync.dma_start(offsets[:], offs)
         nodes = held.tile([P, NODES], BF16, name="nodes")
         nc.sync.dma_start(nodes[:], table)
+        bias = held.tile([P, 2], F32, name="bias")
+        with nc.allow_non_contiguous_dma(reason="256 bias values, one to a partition and column"):
+            nc.scalar.dma_start(bias[:], b.rearrange("(h m) o -> m (h o)", h=2))
         weights = held.tile([P, 2 * P], BF16, name="weights")
         nc.scalar.dma_start(weights[:], w)
-        cell_bias = held.tile([P, 1], F32, name="cell_bias")
-        nc.scalar.dma_start(cell_bias[:], b[0:P, :])
-        gate_bias = held.tile([P, 1], F32, name="gate_bias")
-        nc.sync.dma_start(gate_bias[:], b[P : 2 * P, :])
 
         scratch = held.tile([P, 1], F32, name="scratch")
         nc.vector.memset(scratch[:], 0.0)
@@ -38,12 +37,12 @@ def tile_logicencoder_kernel(tc, table, w, b, offs, out):
         nc.tensor.matmul(gate_sum[:], weights[:, P : 2 * P], nodes[:].indirect(offsets[:]), start=True, stop=True)
 
         squashed = held.tile([P, LEAVES], F32, name="squashed")
-        nc.scalar.activation(squashed[:], cell_sum[:], TANH, bias=cell_bias[:])
+        nc.scalar.activation(squashed[:], cell_sum[:], TANH, bias=bias[:, 0:1])
         cell = held.tile([P, LEAVES], F32, name="cell")
-        nc.scalar.activation(cell[:], cell_sum[:], IDENTITY, bias=cell_bias[:])
+        nc.scalar.activation(cell[:], cell_sum[:], IDENTITY, bias=bias[:, 0:1])
         nc.sync.dma_start(out[0:P, :], cell[:])
         gate = held.tile([P, LEAVES], F32, name="gate")
-        nc.scalar.activation(gate[:], gate_sum[:], SIGMOID, bias=gate_bias[:])
+        nc.scalar.activation(gate[:], gate_sum[:], SIGMOID, bias=bias[:, 1:2])
 
         hidden = held.tile([P, LEAVES], F32, name="hidden")
         nc.vector.tensor_mul(hidden[:], gate[:], squashed[:])

@@ -17,15 +17,15 @@ def tile_logicencoder_kernel(tc, table, w, b, offs, out):
         tc.tile_pool(name="held", bufs=1) as held,
         tc.psum_pool(name="psum", bufs=1) as psum,
     ):
-        offsets = held.tile([P, LEAVES // 16], U16, name="offsets")
-        nc.sync.dma_start(offsets[:], offs)
         nodes = held.tile([P, NODES], BF16, name="nodes")
         nc.sync.dma_start(nodes[:], table)
+        offsets = held.tile([P, LEAVES // 16], U16, name="offsets")
+        nc.sync.dma_start(offsets[:], offs)
+        weights = held.tile([P, 2 * P], BF16, name="weights")
+        nc.scalar.dma_start(weights[:], w)
         bias = held.tile([P, 2], F32, name="bias")
         with nc.allow_non_contiguous_dma(reason="256 bias values, one to a partition and column"):
             nc.scalar.dma_start(bias[:], b.rearrange("(h m) o -> m (h o)", h=2))
-        weights = held.tile([P, 2 * P], BF16, name="weights")
-        nc.scalar.dma_start(weights[:], w)
 
         scratch = held.tile([P, 1], F32, name="scratch")
         nc.vector.memset(scratch[:], 0.0)

@@ -31,19 +31,19 @@ def tile_logicencoder_kernel(tc, table, w, b, offs, out):
         nc.vector.memset(scratch[:], 0.0)
         nc.scalar.activation(scratch[:], scratch[:], SIGMOID)
 
-        cell_sum = psum.tile([P, LEAVES], F32, name="cell_sum")
-        nc.tensor.matmul(cell_sum[:], weights[:, 0:P], nodes[:].indirect(offsets[:]), start=True, stop=True)
         gate_sum = psum.tile([P, LEAVES], F32, name="gate_sum")
         nc.tensor.matmul(gate_sum[:], weights[:, P : 2 * P], nodes[:].indirect(offsets[:]), start=True, stop=True)
+        cell_sum = psum.tile([P, LEAVES], F32, name="cell_sum")
+        nc.tensor.matmul(cell_sum[:], weights[:, 0:P], nodes[:].indirect(offsets[:]), start=True, stop=True)
 
-        squashed = held.tile([P, LEAVES], F32, name="squashed")
-        nc.scalar.activation(squashed[:], cell_sum[:], TANH, bias=bias[:, 0:1])
-        cell = held.tile([P, LEAVES], F32, name="cell")
-        nc.scalar.activation(cell[:], cell_sum[:], IDENTITY, bias=bias[:, 0:1])
-        nc.sync.dma_start(out[0:P, :], cell[:])
         gate = held.tile([P, LEAVES], F32, name="gate")
         nc.scalar.activation(gate[:], gate_sum[:], SIGMOID, bias=bias[:, 1:2])
+        squashed = held.tile([P, LEAVES], F32, name="squashed")
+        nc.scalar.activation(squashed[:], cell_sum[:], TANH, bias=bias[:, 0:1])
 
         hidden = held.tile([P, LEAVES], F32, name="hidden")
         nc.vector.tensor_mul(hidden[:], gate[:], squashed[:])
         nc.sync.dma_start(out[P : 2 * P, :], hidden[:])
+        cell = held.tile([P, LEAVES], F32, name="cell")
+        nc.scalar.activation(cell[:], cell_sum[:], IDENTITY, bias=bias[:, 0:1])
+        nc.sync.dma_start(out[0:P, :], cell[:])

@@ -41,9 +41,9 @@ def tile_logicencoder_kernel(tc, table, w, b, offs, out):
         squashed = held.tile([P, LEAVES], F32, name="squashed")
         nc.scalar.activation(squashed[:], cell_sum[:], TANH, bias=bias[:, 0:1])
 
-        hidden = held.tile([P, LEAVES], F32, name="hidden")
-        nc.vector.tensor_mul(hidden[:], gate[:], squashed[:])
-        nc.sync.dma_start(out[P : 2 * P, :], hidden[:])
         cell = held.tile([P, LEAVES], F32, name="cell")
         nc.scalar.activation(cell[:], cell_sum[:], IDENTITY, bias=bias[:, 0:1])
         nc.sync.dma_start(out[0:P, :], cell[:])
+        hidden = held.tile([P, LEAVES], F32, name="hidden")
+        nc.vector.tensor_mul(hidden[:], gate[:], squashed[:])
+        nc.sync.dma_start(out[P : 2 * P, :], hidden[:])

@@ -8,6 +8,7 @@ IDENTITY = mybir.ActivationFunctionType.Identity
 P = 128
 NODES = 256
 LEAVES = 128
+DMA_ALIGN = 256
 FLOPS = 2 * P * (2 * P) * LEAVES
 
 
@@ -17,11 +18,11 @@ def tile_logicencoder_kernel(tc, table, w, b, offs, out):
         tc.tile_pool(name="held", bufs=1) as held,
         tc.psum_pool(name="psum", bufs=1) as psum,
     ):
-        nodes = held.tile([P, NODES], BF16, name="nodes")
+        nodes = held.tile([P, NODES], BF16, name="nodes", align_bytes=DMA_ALIGN)
         nc.sync.dma_start(nodes[:], table)
         offsets = held.tile([P, LEAVES // 16], U16, name="offsets")
         nc.sync.dma_start(offsets[:], offs)
-        weights = held.tile([P, 2 * P], BF16, name="weights")
+        weights = held.tile([P, 2 * P], BF16, name="weights", align_bytes=DMA_ALIGN)
         nc.scalar.dma_start(weights[:], w)
         bias = held.tile([P, 2], F32, name="bias")
         with nc.allow_non_contiguous_dma(reason="256 bias values, one to a partition and column"):
@@ -41,9 +42,9 @@ def tile_logicencoder_kernel(tc, table, w, b, offs, out):
         squashed = held.tile([P, LEAVES], F32, name="squashed")
         nc.scalar.activation(squashed[:], cell_sum[:], TANH, bias=bias[:, 0:1])
 
-        cell = held.tile([P, LEAVES], F32, name="cell")
+        cell = held.tile([P, LEAVES], F32, name="cell", align_bytes=DMA_ALIGN)
         nc.scalar.activation(cell[:], cell_sum[:], IDENTITY, bias=bias[:, 0:1])
         nc.sync.dma_start(out[0:P, :], cell[:])
-        hidden = held.tile([P, LEAVES], F32, name="hidden")
+        hidden = held.tile([P, LEAVES], F32, name="hidden", align_bytes=DMA_ALIGN)
         nc.vector.tensor_mul(hidden[:], gate[:], squashed[:])
         nc.sync.dma_start(out[P : 2 * P, :], hidden[:])

@@ -8,7 +8,7 @@ IDENTITY = mybir.ActivationFunctionType.Identity
 P = 128
 NODES = 256
 LEAVES = 128
-DMA_ALIGN = 256
+DMA_ALIGN = 512
 FLOPS = 2 * P * (2 * P) * LEAVES
 
 

import concourse.mybir as mybir

BF16, F32, U16 = mybir.dt.bfloat16, mybir.dt.float32, mybir.dt.uint16
SIGMOID = mybir.ActivationFunctionType.Sigmoid
TANH = mybir.ActivationFunctionType.Tanh
IDENTITY = mybir.ActivationFunctionType.Identity

P = 128
NODES = 256
LEAVES = 128
DMA_ALIGN = 512
FLOPS = 2 * P * (2 * P) * LEAVES


def tile_logicencoder_kernel(tc, table, w, b, offs, out):
    nc = tc.nc
    with (
        tc.tile_pool(name="held", bufs=1) as held,
        tc.psum_pool(name="psum", bufs=1) as psum,
    ):
        nodes = held.tile([P, NODES], BF16, name="nodes", align_bytes=DMA_ALIGN)
        nc.sync.dma_start(nodes[:], table)
        offsets = held.tile([P, LEAVES // 16], U16, name="offsets")
        nc.sync.dma_start(offsets[:], offs)
        weights = held.tile([P, 2 * P], BF16, name="weights", align_bytes=DMA_ALIGN)
        nc.scalar.dma_start(weights[:], w)
        bias = held.tile([P, 2], F32, name="bias")
        with nc.allow_non_contiguous_dma(reason="256 bias values, one to a partition and column"):
            nc.scalar.dma_start(bias[:], b.rearrange("(h m) o -> m (h o)", h=2))

        scratch = held.tile([P, 1], F32, name="scratch")
        nc.vector.memset(scratch[:], 0.0)
        nc.scalar.activation(scratch[:], scratch[:], SIGMOID)

        gate_sum = psum.tile([P, LEAVES], F32, name="gate_sum")
        nc.tensor.matmul(gate_sum[:], weights[:, P : 2 * P], nodes[:].indirect(offsets[:]), start=True, stop=True)
        cell_sum = psum.tile([P, LEAVES], F32, name="cell_sum")
        nc.tensor.matmul(cell_sum[:], weights[:, 0:P], nodes[:].indirect(offsets[:]), start=True, stop=True)

        gate = held.tile([P, LEAVES], F32, name="gate")
        nc.scalar.activation(gate[:], gate_sum[:], SIGMOID, bias=bias[:, 1:2])
        squashed = held.tile([P, LEAVES], F32, name="squashed")
        nc.scalar.activation(squashed[:], cell_sum[:], TANH, bias=bias[:, 0:1])

        cell = held.tile([P, LEAVES], F32, name="cell", align_bytes=DMA_ALIGN)
        nc.scalar.activation(cell[:], cell_sum[:], IDENTITY, bias=bias[:, 0:1])
        nc.sync.dma_start(out[0:P, :], cell[:])
        hidden = held.tile([P, LEAVES], F32, name="hidden", align_bytes=DMA_ALIGN)
        nc.vector.tensor_mul(hidden[:], gate[:], squashed[:])
        nc.sync.dma_start(out[P : 2 * P, :], hidden[:])
